import numpy as np
import ml_dtypes


def mxq(x, axis, fmt="e4m3"):
    dtype, down = {"e4m3": (ml_dtypes.float8_e4m3fn, 7), "e5m2": (ml_dtypes.float8_e5m2, 14)}[fmt]
    v = np.moveaxis(np.asarray(x, np.float32).astype(ml_dtypes.bfloat16).astype(np.float64), axis, -1)
    blocks = v.reshape(v.shape[:-1] + (-1, 32))
    amax = np.abs(blocks).max(-1, keepdims=True)
    byte = np.maximum(np.where(amax > 0, np.frexp(amax)[1] - 1 + 127, 0) - down, 1)
    scale = np.exp2(byte - 127.0)
    codes = (blocks / scale).astype(np.float32).astype(dtype).astype(np.float64)
    return np.moveaxis((codes * scale).reshape(v.shape), -1, axis)


WIDE = False


def mx_kscale(k):
    if not WIDE:
        return np.ones(k)
    levels = np.array([10, -10, 5, -5, 0])
    a = np.random.permutation(np.resize(levels, k // 512 * 4)).reshape(k // 512, 4)
    idx = np.arange(k)
    return np.exp2(a[idx // 512, idx % 128 // 32])


BF16 = ml_dtypes.bfloat16


def bf(x):
    return np.asarray(x, np.float32).astype(BF16)


def f64(x):
    return np.asarray(x).astype(np.float64)


B, R, RS, RED, F1, F2, NC = 8192, 64, 60, 16, 128, 512, 256
C = R * RED
EPS = 1e-5
SLOPE = 0.3


def bn_train(h, gamma, beta):
    mean = h.mean(axis=0)
    var = h.var(axis=0)
    return (h - mean) * (1.0 / np.sqrt(var + EPS)) * gamma + beta


def setup_inputs():
    s = mx_kscale(C)
    sr = s.reshape(R, RED)
    sig = np.exp2(np.random.uniform(-8.0, 1.0, (R, RED)))
    off = 0.7 * np.random.standard_normal((R, RED))
    return {"h_enc": bf((np.random.standard_normal((B, R, RED)) + off) * sig),
            "enc_gamma": bf((1.0 + 0.1 * np.random.standard_normal((R, RED))) * sr),
            "enc_beta": bf(0.3 * np.random.standard_normal((R, RED)) * sr),
            "w1": bf(np.random.standard_normal((F1, C)) / np.sqrt(C) / s[None, :]),
            "b1": bf(0.3 * np.random.standard_normal(F1))}


def reference(h_enc, enc_gamma, enc_beta, w1, b1):
    h = bn_train(f64(h_enc), f64(enc_gamma), f64(enc_beta))
    h = np.where(h >= 0, h, SLOPE * h)
    c = h.reshape(B, C)
    return (mxq(c, 1, "e4m3") @ mxq(f64(w1), 1, "e4m3").T) + f64(b1)

@@ -1,0 +1,247 @@
+from contextlib import ExitStack
+
+import concourse.mybir as mybir
+from concourse.masks import make_identity
+
+F32 = mybir.dt.float32
+BF16 = mybir.dt.bfloat16
+U32 = mybir.dt.uint32
+U8 = mybir.dt.uint8
+FP8X4 = mybir.dt.float8_e4m3fn_x4
+ALU = mybir.AluOpType
+ACT = mybir.ActivationFunctionType
+
+P = 128
+BATCH = 8192
+CHANNELS = 1024
+FEATURES = 128
+EPS = 1e-5
+SLOPE = 0.3
+
+ROW_TILES = 4
+CHUNK = P * ROW_TILES
+CHUNKS = BATCH // CHUNK
+WORDS = CHANNELS // 2
+SLABS = WORDS // P
+PASSES = 2
+PLANES = 2 * SLABS
+BN_WIDTH = 512
+
+FLOPS = 2 * BATCH * CHANNELS * FEATURES
+
+
+def transpose_slab(nc, bank, x_chunk, slab, ident):
+    for j in range(ROW_TILES):
+        nc.tensor.transpose(
+            out=bank[:, j * P : (j + 1) * P],
+            in_=x_chunk[:, j, :].bitcast(F32)[:, slab * P : (slab + 1) * P],
+            identity=ident[:],
+        )
+
+
+def half(bank, e):
+    return bank[:].bitcast(BF16).rearrange("p (b e) -> p b e", e=2)[:, :, e]
+
+
+def tile_roibaseline_pa_t_kernel(tc, h_enc, enc_gamma, enc_beta, w1, b1, out):
+    nc = tc.nc
+    with ExitStack() as ctx:
+        keep = ctx.enter_context(tc.tile_pool(name="keep", bufs=1))
+        junk_pool = ctx.enter_context(tc.tile_pool(name="junk", bufs=4))
+        y_pool = ctx.enter_context(tc.tile_pool(name="y", bufs=3))
+        c_pool = ctx.enter_context(tc.tile_pool(name="c", bufs=3))
+        q_pool = ctx.enter_context(tc.tile_pool(name="q", bufs=3))
+        o_pool = ctx.enter_context(tc.tile_pool(name="o", bufs=3))
+        xt_psum = ctx.enter_context(tc.psum_pool(name="xt", bufs=5))
+        acc_psum = ctx.enter_context(tc.psum_pool(name="acc", bufs=2))
+        sum_psum = ctx.enter_context(tc.psum_pool(name="sum", bufs=1))
+
+        ident = keep.tile([P, P], F32, name="ident")
+        make_identity(nc, ident[:])
+        ones = keep.tile([P, 1], BF16, name="ones")
+        nc.vector.memset(ones[:], 1.0)
+        warm = keep.tile([P, 1], F32, name="warm")
+        nc.vector.memset(warm[:], 1.0)
+        nc.scalar.activation(out=warm[:], in_=warm[:], func=ACT.Sqrt)
+
+        w_rows = keep.tile([P, CHANNELS], BF16, name="w_rows")
+        nc.scalar.dma_start(out=w_rows[:], in_=w1)
+        gamma_bf = keep.tile([P, SLABS, 2], BF16, name="gamma_bf")
+        beta_bf = keep.tile([P, SLABS, 2], BF16, name="beta_bf")
+        nc.scalar.dma_start(
+            out=gamma_bf[:],
+            in_=enc_gamma.rearrange("r o -> (r o)").rearrange("(s p e) -> p s e", s=SLABS, p=P),
+        )
+        nc.scalar.dma_start(
+            out=beta_bf[:],
+            in_=enc_beta.rearrange("r o -> (r o)").rearrange("(s p e) -> p s e", s=SLABS, p=P),
+        )
+        bias_bf = keep.tile([P, FEATURES], BF16, name="bias_bf")
+        nc.scalar.dma_start(out=bias_bf[:], in_=b1.partition_broadcast(P))
+
+        x_chunks = []
+        for c in range(CHUNKS):
+            x_chunk = keep.tile([P, ROW_TILES, CHANNELS], BF16, name="x%d" % c)
+            nc.sync.dma_start(
+                out=x_chunk[:],
+                in_=h_enc[c * CHUNK : (c + 1) * CHUNK].rearrange(
+                    "(p j) r o -> p j (r o)", j=ROW_TILES
+                ),
+            )
+            x_chunks.append(x_chunk)
+
+        gamma = keep.tile([P, PLANES], F32, name="gamma")
+        beta = keep.tile([P, PLANES], F32, name="beta")
+        bias = keep.tile([P, FEATURES], F32, name="bias")
+        nc.vector.tensor_copy(out=gamma[:], in_=gamma_bf[:].rearrange("p s e -> p (s e)"))
+        nc.vector.tensor_copy(out=beta[:], in_=beta_bf[:].rearrange("p s e -> p (s e)"))
+        nc.vector.tensor_copy(out=bias[:], in_=bias_bf[:])
+
+        w_bank = xt_psum.tile([P, SLABS * P], F32, tag="xt", name="w_bank")
+        for s in range(SLABS):
+            nc.tensor.transpose(
+                out=w_bank[:, s * P : (s + 1) * P],
+                in_=w_rows[:].bitcast(F32)[:, s * P : (s + 1) * P],
+                identity=ident[:],
+            )
+        w_grouped = keep.tile([P, PASSES * FEATURES * 4], BF16, name="w_grouped", align_bytes=64)
+        nc.vector.tensor_copy(
+            out=w_grouped[:].bitcast(F32).rearrange("p (g f u) -> p g f u", g=PASSES, u=2),
+            in_=w_bank[:].rearrange("p (g u f) -> p g f u", g=PASSES, u=2),
+        )
+        w_codes = keep.tile([P, PASSES * FEATURES], U32, name="w_codes", align_bytes=64)
+        w_scales = keep.tile([P, PASSES * FEATURES], U8, name="w_scales", align_bytes=64)
+        nc.vector.quantize_mx(out=w_codes[:].bitcast(FP8X4), scales=w_scales[:], in_=w_grouped[:])
+
+        halves = CHUNK * 2 // BN_WIDTH
+        bn_parts = keep.tile([P, 2, CHUNKS * halves, 6], F32, name="bn_parts")
+        neg_x0 = keep.tile([P, 4], F32, name="neg_x0")
+        sq_parts = keep.tile([P, 4, CHUNKS], F32, name="sq_parts")
+        sum_parts = sum_psum.tile([P, 4, CHUNKS], F32, name="sum_parts")
+        for c in range(CHUNKS):
+            for s in range(SLABS):
+                bank = xt_psum.tile([P, CHUNK], F32, tag="xt", name="bank_a")
+                transpose_slab(nc, bank, x_chunks[c], s, ident)
+                if s < 2:
+                    for h in range(halves):
+                        nc.vector.bn_stats(
+                            out=bn_parts[:, s, c * halves + h, :],
+                            in_=bank[:].bitcast(BF16)[:, h * BN_WIDTH : (h + 1) * BN_WIDTH],
+                        )
+                else:
+                    u = s - 2
+                    if c == 0:
+                        nc.scalar.mul(
+                            out=neg_x0[:, 2 * u : 2 * u + 2],
+                            in_=bank[:].bitcast(BF16)[:, 0:2],
+                            mul=-1.0,
+                        )
+                    for e in range(2):
+                        junk = junk_pool.tile([P, CHUNK], BF16, name="junk")
+                        nc.scalar.activation(
+                            out=junk[:],
+                            in_=half(bank, e),
+                            func=ACT.Square,
+                            bias=neg_x0[:, 2 * u + e : 2 * u + e + 1],
+                            scale=1.0,
+                            accum_out=sq_parts[:, 2 * u + e, c : c + 1],
+                        )
+            for v in range(4):
+                first = CHANNELS // 2 + 256 * (v // 2) + v % 2
+                for j in range(ROW_TILES):
+                    nc.tensor.matmul(
+                        out=sum_parts[:, v, c : c + 1],
+                        lhsT=x_chunks[c][:, j, first : first + 255 : 2],
+                        rhs=ones[:],
+                        start=(j == 0),
+                        stop=(j == ROW_TILES - 1),
+                    )
+
+        mean_var = keep.tile([P, PLANES, 2], F32, name="mean_var")
+        for s in range(2):
+            for e in range(2):
+                nc.vector.bn_aggr(
+                    out=mean_var[:, 2 * s + e, :], in_=bn_parts[:, s, :, 3 * e : 3 * e + 3]
+                )
+        x_sum = keep.tile([P, 4], F32, name="x_sum")
+        sq_sum = keep.tile([P, 4], F32, name="sq_sum")
+        nc.vector.tensor_reduce(out=x_sum[:], in_=sum_parts[:], axis=mybir.AxisListType.X, op=ALU.add)
+        nc.vector.tensor_reduce(out=sq_sum[:], in_=sq_parts[:], axis=mybir.AxisListType.X, op=ALU.add)
+        nc.vector.tensor_scalar_mul(out=mean_var[:, 4:8, 0], in0=x_sum[:], scalar1=1.0 / BATCH)
+        off = keep.tile([P, 4], F32, name="off")
+        nc.vector.tensor_add(out=off[:], in0=mean_var[:, 4:8, 0], in1=neg_x0[:])
+        nc.vector.tensor_mul(out=off[:], in0=off[:], in1=off[:])
+        nc.vector.scalar_tensor_tensor(
+            out=mean_var[:, 4:8, 1],
+            in0=sq_sum[:],
+            scalar=1.0 / BATCH,
+            in1=off[:],
+            op0=ALU.mult,
+            op1=ALU.subtract,
+        )
+        std = keep.tile([P, PLANES], F32, name="std")
+        nc.vector.tensor_scalar_add(out=std[:], in0=mean_var[:, :, 1], scalar1=EPS)
+        nc.scalar.activation(out=std[:], in_=std[:], func=ACT.Sqrt)
+        scale = keep.tile([P, PLANES], F32, name="scale")
+        shift = keep.tile([P, PLANES], F32, name="shift")
+        nc.vector.reciprocal(out=scale[:], in_=std[:])
+        nc.vector.tensor_mul(out=scale[:], in0=scale[:], in1=gamma[:])
+        nc.vector.tensor_mul(out=shift[:], in0=mean_var[:, :, 0], in1=scale[:])
+        nc.vector.tensor_sub(out=shift[:], in0=beta[:], in1=shift[:])
+
+        for c in range(CHUNKS):
+            codes = q_pool.tile([P, PASSES, CHUNK], U32, name="codes", align_bytes=64)
+            scales = q_pool.tile([P, PASSES, CHUNK], U8, name="scales", align_bytes=64)
+            for g in range(PASSES):
+                y = y_pool.tile([P, 4, CHUNK], F32, name="y")
+                for u in range(2):
+                    s = 2 * g + u
+                    bank = xt_psum.tile([P, CHUNK], F32, tag="xt", name="bank_b")
+                    transpose_slab(nc, bank, x_chunks[c], s, ident)
+                    for e in range(2):
+                        nc.scalar.activation(
+                            out=y[:, 2 * u + e, :],
+                            in_=half(bank, e),
+                            func=ACT.Identity,
+                            bias=shift[:, 2 * s + e : 2 * s + e + 1],
+                            scale=scale[:, 2 * s + e : 2 * s + e + 1],
+                        )
+                grouped = c_pool.tile([P, CHUNK, 4], BF16, name="grouped", align_bytes=64)
+                y_by_row = y[:].rearrange("p t b -> p b t")
+                nc.vector.scalar_tensor_tensor(
+                    out=grouped[:],
+                    in0=y_by_row,
+                    scalar=SLOPE,
+                    in1=y_by_row,
+                    op0=ALU.mult,
+                    op1=ALU.max,
+                )
+                nc.vector.quantize_mx(
+                    out=codes[:, g, :].bitcast(FP8X4),
+                    scales=scales[:, g, :],
+                    in_=grouped[:].rearrange("p b t -> p (b t)"),
+                )
+            acc = acc_psum.tile([P, ROW_TILES, FEATURES], F32, name="acc")
+            for j in range(ROW_TILES):
+                rows = slice(j * P, (j + 1) * P)
+                for g in range(PASSES):
+                    cols = slice(g * FEATURES, (g + 1) * FEATURES)
+                    nc.tensor.matmul_mx(
+                        out=acc[:, j, :],
+                        lhsT=codes[:, g, rows].bitcast(FP8X4),
+                        lhsT_scale=scales[:, g, rows],
+                        rhs=w_codes[:, cols].bitcast(FP8X4),
+                        rhs_scale=w_scales[:, cols],
+                        start=(g == 0),
+                        stop=(g == PASSES - 1),
+                    )
+            result = o_pool.tile([P, ROW_TILES, FEATURES], F32, name="result")
+            nc.vector.tensor_add(
+                out=result[:],
+                in0=acc[:],
+                in1=bias[:].unsqueeze(1).to_broadcast([P, ROW_TILES, FEATURES]),
+            )
+            nc.sync.dma_start(
+                out=out[c * CHUNK : (c + 1) * CHUNK, :].rearrange("(p j) f -> p j f", j=ROW_TILES),
+                in_=result[:],
+            )

@@ -48,8 +48,9 @@ def tile_roibaseline_pa_t_kernel(tc, h_enc, enc_gamma, enc_beta, w1, b1, out):
     with ExitStack() as ctx:
         keep = ctx.enter_context(tc.tile_pool(name="keep", bufs=1))
         junk_pool = ctx.enter_context(tc.tile_pool(name="junk", bufs=4))
-        y_pool = ctx.enter_context(tc.tile_pool(name="y", bufs=3))
-        c_pool = ctx.enter_context(tc.tile_pool(name="c", bufs=3))
+        xt_pool = ctx.enter_context(tc.tile_pool(name="xts", bufs=3))
+        y_pool = ctx.enter_context(tc.tile_pool(name="y", bufs=2))
+        c_pool = ctx.enter_context(tc.tile_pool(name="c", bufs=2))
         q_pool = ctx.enter_context(tc.tile_pool(name="q", bufs=3))
         o_pool = ctx.enter_context(tc.tile_pool(name="o", bufs=3))
         xt_psum = ctx.enter_context(tc.psum_pool(name="xt", bufs=5))
@@ -58,6 +59,8 @@ def tile_roibaseline_pa_t_kernel(tc, h_enc, enc_gamma, enc_beta, w1, b1, out):
 
         ident = keep.tile([P, P], F32, name="ident")
         make_identity(nc, ident[:])
+        ident_bf = keep.tile([P, P], BF16, name="ident_bf")
+        make_identity(nc, ident_bf[:])
         ones = keep.tile([P, 1], BF16, name="ones")
         nc.vector.memset(ones[:], 1.0)
         warm = keep.tile([P, 1], F32, name="warm")
@@ -189,37 +192,56 @@ def tile_roibaseline_pa_t_kernel(tc, h_enc, enc_gamma, enc_beta, w1, b1, out):
         nc.vector.tensor_mul(out=shift[:], in0=mean_var[:, :, 0], in1=scale[:])
         nc.vector.tensor_sub(out=shift[:], in0=beta[:], in1=shift[:])
 
+        scale_neg = keep.tile([P, PLANES], F32, name="scale_neg")
+        shift_neg = keep.tile([P, PLANES], F32, name="shift_neg")
+        nc.vector.tensor_scalar_mul(out=scale_neg[:], in0=scale[:], scalar1=SLOPE)
+        nc.vector.tensor_scalar_mul(out=shift_neg[:], in0=shift[:], scalar1=SLOPE)
+
         for c in range(CHUNKS):
+            x_planes = xt_pool.tile([P, PLANES, CHUNK], BF16, name="x_planes")
+            for s in range(SLABS):
+                bank = xt_psum.tile([P, 2, CHUNK], BF16, tag="xt", name="bank_b")
+                for e in range(2):
+                    first = 256 * s + e
+                    for j in range(ROW_TILES):
+                        nc.tensor.transpose(
+                            out=bank[:, e, j * P : (j + 1) * P],
+                            in_=x_chunks[c][:, j, first : first + 255 : 2],
+                            identity=ident_bf[:],
+                        )
+                nc.scalar.copy(out=x_planes[:, 2 * s : 2 * s + 2, :], in_=bank[:])
+            y_pos = y_pool.tile([P, PLANES, CHUNK], BF16, name="y_pos")
+            for v in range(PLANES):
+                nc.vector.tensor_scalar(
+                    out=y_pos[:, v, :],
+                    in0=x_planes[:, v, :],
+                    scalar1=scale[:, v : v + 1],
+                    scalar2=shift[:, v : v + 1],
+                    op0=ALU.mult,
+                    op1=ALU.add,
+                )
+                nc.vector.tensor_scalar(
+                    out=x_planes[:, v, :],
+                    in0=x_planes[:, v, :],
+                    scalar1=scale_neg[:, v : v + 1],
+                    scalar2=shift_neg[:, v : v + 1],
+                    op0=ALU.mult,
+                    op1=ALU.add,
+                )
+            nc.vector.tensor_max(out=x_planes[:], in0=y_pos[:], in1=x_planes[:])
+            grouped = c_pool.tile([P, PASSES, CHUNK, 4], BF16, name="grouped", align_bytes=64)
+            for g in range(PASSES):
+                nc.scalar.copy(
+                    out=grouped[:, g, :, :].rearrange("p (n i) t -> p n t i", i=4),
+                    in_=x_planes[:, 4 * g : 4 * g + 4, :].rearrange("p t (n i) -> p n t i", i=4),
+                )
             codes = q_pool.tile([P, PASSES, CHUNK], U32, name="codes", align_bytes=64)
             scales = q_pool.tile([P, PASSES, CHUNK], U8, name="scales", align_bytes=64)
             for g in range(PASSES):
-                y = y_pool.tile([P, 4, CHUNK], F32, name="y")
-                for u in range(2):
-                    s = 2 * g + u
-                    bank = xt_psum.tile([P, CHUNK], F32, tag="xt", name="bank_b")
-                    transpose_slab(nc, bank, x_chunks[c], s, ident)
-                    for e in range(2):
-                        nc.scalar.activation(
-                            out=y[:, 2 * u + e, :],
-                            in_=half(bank, e),
-                            func=ACT.Identity,
-                            bias=shift[:, 2 * s + e : 2 * s + e + 1],
-                            scale=scale[:, 2 * s + e : 2 * s + e + 1],
-                        )
-                grouped = c_pool.tile([P, CHUNK, 4], BF16, name="grouped", align_bytes=64)
-                y_by_row = y[:].rearrange("p t b -> p b t")
-                nc.vector.scalar_tensor_tensor(
-                    out=grouped[:],
-                    in0=y_by_row,
-                    scalar=SLOPE,
-                    in1=y_by_row,
-                    op0=ALU.mult,
-                    op1=ALU.max,
-                )
                 nc.vector.quantize_mx(
                     out=codes[:, g, :].bitcast(FP8X4),
                     scales=scales[:, g, :],
-                    in_=grouped[:].rearrange("p b t -> p (b t)"),
+                    in_=grouped[:, g, :, :].rearrange("p b t -> p (b t)"),
                 )
             acc = acc_psum.tile([P, ROW_TILES, FEATURES], F32, name="acc")
             for j in range(ROW_TILES):

@@ -26,6 +26,7 @@ SLABS = WORDS // P
 PASSES = 2
 PLANES = 2 * SLABS
 BN_WIDTH = 512
+V_SLABS = 3
 
 FLOPS = 2 * BATCH * CHANNELS * FEATURES
 
@@ -48,21 +49,15 @@ def tile_roibaseline_pa_t_kernel(tc, h_enc, enc_gamma, enc_beta, w1, b1, out):
     with ExitStack() as ctx:
         keep = ctx.enter_context(tc.tile_pool(name="keep", bufs=1))
         junk_pool = ctx.enter_context(tc.tile_pool(name="junk", bufs=4))
-        xt_pool = ctx.enter_context(tc.tile_pool(name="xts", bufs=3))
-        y_pool = ctx.enter_context(tc.tile_pool(name="y", bufs=2))
-        c_pool = ctx.enter_context(tc.tile_pool(name="c", bufs=2))
+        y_pool = ctx.enter_context(tc.tile_pool(name="y", bufs=3))
+        c_pool = ctx.enter_context(tc.tile_pool(name="c", bufs=3))
         q_pool = ctx.enter_context(tc.tile_pool(name="q", bufs=3))
         o_pool = ctx.enter_context(tc.tile_pool(name="o", bufs=3))
-        xt_psum = ctx.enter_context(tc.psum_pool(name="xt", bufs=5))
+        xt_psum = ctx.enter_context(tc.psum_pool(name="xt", bufs=6))
         acc_psum = ctx.enter_context(tc.psum_pool(name="acc", bufs=2))
-        sum_psum = ctx.enter_context(tc.psum_pool(name="sum", bufs=1))
 
         ident = keep.tile([P, P], F32, name="ident")
         make_identity(nc, ident[:])
-        ident_bf = keep.tile([P, P], BF16, name="ident_bf")
-        make_identity(nc, ident_bf[:])
-        ones = keep.tile([P, 1], BF16, name="ones")
-        nc.vector.memset(ones[:], 1.0)
         warm = keep.tile([P, 1], F32, name="warm")
         nc.vector.memset(warm[:], 1.0)
         nc.scalar.activation(out=warm[:], in_=warm[:], func=ACT.Sqrt)
@@ -117,68 +112,53 @@ def tile_roibaseline_pa_t_kernel(tc, h_enc, enc_gamma, enc_beta, w1, b1, out):
         nc.vector.quantize_mx(out=w_codes[:].bitcast(FP8X4), scales=w_scales[:], in_=w_grouped[:])
 
         halves = CHUNK * 2 // BN_WIDTH
-        bn_parts = keep.tile([P, 2, CHUNKS * halves, 6], F32, name="bn_parts")
-        neg_x0 = keep.tile([P, 4], F32, name="neg_x0")
-        sq_parts = keep.tile([P, 4, CHUNKS], F32, name="sq_parts")
-        sum_parts = sum_psum.tile([P, 4, CHUNKS], F32, name="sum_parts")
+        bn_parts = keep.tile([P, V_SLABS, CHUNKS * halves, 6], F32, name="bn_parts")
+        neg_x0 = keep.tile([P, 2], F32, name="neg_x0")
+        d_parts = keep.tile([P, 2, CHUNKS], F32, name="d_parts")
+        dd_parts = keep.tile([P, 2, CHUNKS], F32, name="dd_parts")
         for c in range(CHUNKS):
             for s in range(SLABS):
                 bank = xt_psum.tile([P, CHUNK], F32, tag="xt", name="bank_a")
                 transpose_slab(nc, bank, x_chunks[c], s, ident)
-                if s < 2:
+                if s < V_SLABS:
                     for h in range(halves):
                         nc.vector.bn_stats(
                             out=bn_parts[:, s, c * halves + h, :],
                             in_=bank[:].bitcast(BF16)[:, h * BN_WIDTH : (h + 1) * BN_WIDTH],
                         )
                 else:
-                    u = s - 2
                     if c == 0:
-                        nc.scalar.mul(
-                            out=neg_x0[:, 2 * u : 2 * u + 2],
-                            in_=bank[:].bitcast(BF16)[:, 0:2],
-                            mul=-1.0,
-                        )
+                        nc.scalar.mul(out=neg_x0[:], in_=bank[:].bitcast(BF16)[:, 0:2], mul=-1.0)
                     for e in range(2):
-                        junk = junk_pool.tile([P, CHUNK], BF16, name="junk")
-                        nc.scalar.activation(
-                            out=junk[:],
-                            in_=half(bank, e),
-                            func=ACT.Square,
-                            bias=neg_x0[:, 2 * u + e : 2 * u + e + 1],
-                            scale=1.0,
-                            accum_out=sq_parts[:, 2 * u + e, c : c + 1],
-                        )
-            for v in range(4):
-                first = CHANNELS // 2 + 256 * (v // 2) + v % 2
-                for j in range(ROW_TILES):
-                    nc.tensor.matmul(
-                        out=sum_parts[:, v, c : c + 1],
-                        lhsT=x_chunks[c][:, j, first : first + 255 : 2],
-                        rhs=ones[:],
-                        start=(j == 0),
-                        stop=(j == ROW_TILES - 1),
-                    )
+                        for func, parts in ((ACT.Identity, d_parts), (ACT.Square, dd_parts)):
+                            junk = junk_pool.tile([P, CHUNK], BF16, name="junk")
+                            nc.scalar.activation(
+                                out=junk[:],
+                                in_=half(bank, e),
+                                func=func,
+                                bias=neg_x0[:, e : e + 1],
+                                scale=1.0,
+                                accum_out=parts[:, e, c : c + 1],
+                            )
 
         mean_var = keep.tile([P, PLANES, 2], F32, name="mean_var")
-        for s in range(2):
+        for s in range(V_SLABS):
             for e in range(2):
                 nc.vector.bn_aggr(
                     out=mean_var[:, 2 * s + e, :], in_=bn_parts[:, s, :, 3 * e : 3 * e + 3]
                 )
-        x_sum = keep.tile([P, 4], F32, name="x_sum")
-        sq_sum = keep.tile([P, 4], F32, name="sq_sum")
-        nc.vector.tensor_reduce(out=x_sum[:], in_=sum_parts[:], axis=mybir.AxisListType.X, op=ALU.add)
-        nc.vector.tensor_reduce(out=sq_sum[:], in_=sq_parts[:], axis=mybir.AxisListType.X, op=ALU.add)
-        nc.vector.tensor_scalar_mul(out=mean_var[:, 4:8, 0], in0=x_sum[:], scalar1=1.0 / BATCH)
-        off = keep.tile([P, 4], F32, name="off")
-        nc.vector.tensor_add(out=off[:], in0=mean_var[:, 4:8, 0], in1=neg_x0[:])
-        nc.vector.tensor_mul(out=off[:], in0=off[:], in1=off[:])
+        d_mean = keep.tile([P, 2], F32, name="d_mean")
+        dd_mean = keep.tile([P, 2], F32, name="dd_mean")
+        nc.vector.tensor_reduce(out=d_mean[:], in_=d_parts[:], axis=mybir.AxisListType.X, op=ALU.add)
+        nc.vector.tensor_reduce(out=dd_mean[:], in_=dd_parts[:], axis=mybir.AxisListType.X, op=ALU.add)
+        nc.vector.tensor_scalar_mul(out=d_mean[:], in0=d_mean[:], scalar1=1.0 / BATCH)
+        nc.vector.tensor_sub(out=mean_var[:, 2 * V_SLABS :, 0], in0=d_mean[:], in1=neg_x0[:])
+        nc.vector.tensor_mul(out=d_mean[:], in0=d_mean[:], in1=d_mean[:])
         nc.vector.scalar_tensor_tensor(
-            out=mean_var[:, 4:8, 1],
-            in0=sq_sum[:],
+            out=mean_var[:, 2 * V_SLABS :, 1],
+            in0=dd_mean[:],
             scalar=1.0 / BATCH,
-            in1=off[:],
+            in1=d_mean[:],
             op0=ALU.mult,
             op1=ALU.subtract,
         )
@@ -192,56 +172,37 @@ def tile_roibaseline_pa_t_kernel(tc, h_enc, enc_gamma, enc_beta, w1, b1, out):
         nc.vector.tensor_mul(out=shift[:], in0=mean_var[:, :, 0], in1=scale[:])
         nc.vector.tensor_sub(out=shift[:], in0=beta[:], in1=shift[:])
 
-        scale_neg = keep.tile([P, PLANES], F32, name="scale_neg")
-        shift_neg = keep.tile([P, PLANES], F32, name="shift_neg")
-        nc.vector.tensor_scalar_mul(out=scale_neg[:], in0=scale[:], scalar1=SLOPE)
-        nc.vector.tensor_scalar_mul(out=shift_neg[:], in0=shift[:], scalar1=SLOPE)
-
         for c in range(CHUNKS):
-            x_planes = xt_pool.tile([P, PLANES, CHUNK], BF16, name="x_planes")
-            for s in range(SLABS):
-                bank = xt_psum.tile([P, 2, CHUNK], BF16, tag="xt", name="bank_b")
-                for e in range(2):
-                    first = 256 * s + e
-                    for j in range(ROW_TILES):
-                        nc.tensor.transpose(
-                            out=bank[:, e, j * P : (j + 1) * P],
-                            in_=x_chunks[c][:, j, first : first + 255 : 2],
-                            identity=ident_bf[:],
-                        )
-                nc.scalar.copy(out=x_planes[:, 2 * s : 2 * s + 2, :], in_=bank[:])
-            y_pos = y_pool.tile([P, PLANES, CHUNK], BF16, name="y_pos")
-            for v in range(PLANES):
-                nc.vector.tensor_scalar(
-                    out=y_pos[:, v, :],
-                    in0=x_planes[:, v, :],
-                    scalar1=scale[:, v : v + 1],
-                    scalar2=shift[:, v : v + 1],
-                    op0=ALU.mult,
-                    op1=ALU.add,
-                )
-                nc.vector.tensor_scalar(
-                    out=x_planes[:, v, :],
-                    in0=x_planes[:, v, :],
-                    scalar1=scale_neg[:, v : v + 1],
-                    scalar2=shift_neg[:, v : v + 1],
-                    op0=ALU.mult,
-                    op1=ALU.add,
-                )
-            nc.vector.tensor_max(out=x_planes[:], in0=y_pos[:], in1=x_planes[:])
-            grouped = c_pool.tile([P, PASSES, CHUNK, 4], BF16, name="grouped", align_bytes=64)
-            for g in range(PASSES):
-                nc.scalar.copy(
-                    out=grouped[:, g, :, :].rearrange("p (n i) t -> p n t i", i=4),
-                    in_=x_planes[:, 4 * g : 4 * g + 4, :].rearrange("p t (n i) -> p n t i", i=4),
-                )
             codes = q_pool.tile([P, PASSES, CHUNK], U32, name="codes", align_bytes=64)
             scales = q_pool.tile([P, PASSES, CHUNK], U8, name="scales", align_bytes=64)
             for g in range(PASSES):
+                y = y_pool.tile([P, 4, CHUNK], F32, name="y")
+                for u in range(2):
+                    s = 2 * g + u
+                    bank = xt_psum.tile([P, CHUNK], F32, tag="xt", name="bank_b")
+                    transpose_slab(nc, bank, x_chunks[c], s, ident)
+                    for e in range(2):
+                        nc.scalar.activation(
+                            out=y[:, 2 * u + e, :],
+                            in_=half(bank, e),
+                            func=ACT.Identity,
+                            bias=shift[:, 2 * s + e : 2 * s + e + 1],
+                            scale=scale[:, 2 * s + e : 2 * s + e + 1],
+                        )
+                grouped = c_pool.tile([P, CHUNK, 4], BF16, name="grouped", align_bytes=64)
+                y_by_row = y[:].rearrange("p t b -> p b t")
+                nc.vector.scalar_tensor_tensor(
+                    out=grouped[:],
+                    in0=y_by_row,
+                    scalar=SLOPE,
+                    in1=y_by_row,
+                    op0=ALU.mult,
+                    op1=ALU.max,
+                )
                 nc.vector.quantize_mx(
                     out=codes[:, g, :].bitcast(FP8X4),
                     scales=scales[:, g, :],
-                    in_=grouped[:, g, :, :].rearrange("p b t -> p (b t)"),
+                    in_=grouped[:].rearrange("p b t -> p (b t)"),
                 )
             acc = acc_psum.tile([P, ROW_TILES, FEATURES], F32, name="acc")
             for j in range(ROW_TILES):

@@ -26,7 +26,6 @@ SLABS = WORDS // P
 PASSES = 2
 PLANES = 2 * SLABS
 BN_WIDTH = 512
-V_SLABS = 3
 
 FLOPS = 2 * BATCH * CHANNELS * FEATURES
 
@@ -53,11 +52,14 @@ def tile_roibaseline_pa_t_kernel(tc, h_enc, enc_gamma, enc_beta, w1, b1, out):
         c_pool = ctx.enter_context(tc.tile_pool(name="c", bufs=3))
         q_pool = ctx.enter_context(tc.tile_pool(name="q", bufs=3))
         o_pool = ctx.enter_context(tc.tile_pool(name="o", bufs=3))
-        xt_psum = ctx.enter_context(tc.psum_pool(name="xt", bufs=6))
+        xt_psum = ctx.enter_context(tc.psum_pool(name="xt", bufs=5))
         acc_psum = ctx.enter_context(tc.psum_pool(name="acc", bufs=2))
+        sum_psum = ctx.enter_context(tc.psum_pool(name="sum", bufs=1))
 
         ident = keep.tile([P, P], F32, name="ident")
         make_identity(nc, ident[:])
+        ones = keep.tile([P, 1], BF16, name="ones")
+        nc.vector.memset(ones[:], 1.0)
         warm = keep.tile([P, 1], F32, name="warm")
         nc.vector.memset(warm[:], 1.0)
         nc.scalar.activation(out=warm[:], in_=warm[:], func=ACT.Sqrt)
@@ -112,53 +114,68 @@ def tile_roibaseline_pa_t_kernel(tc, h_enc, enc_gamma, enc_beta, w1, b1, out):
         nc.vector.quantize_mx(out=w_codes[:].bitcast(FP8X4), scales=w_scales[:], in_=w_grouped[:])
 
         halves = CHUNK * 2 // BN_WIDTH
-        bn_parts = keep.tile([P, V_SLABS, CHUNKS * halves, 6], F32, name="bn_parts")
-        neg_x0 = keep.tile([P, 2], F32, name="neg_x0")
-        d_parts = keep.tile([P, 2, CHUNKS], F32, name="d_parts")
-        dd_parts = keep.tile([P, 2, CHUNKS], F32, name="dd_parts")
+        bn_parts = keep.tile([P, 2, CHUNKS * halves, 6], F32, name="bn_parts")
+        neg_x0 = keep.tile([P, 4], F32, name="neg_x0")
+        sq_parts = keep.tile([P, 4, CHUNKS], F32, name="sq_parts")
+        sum_parts = sum_psum.tile([P, 4, CHUNKS], F32, name="sum_parts")
         for c in range(CHUNKS):
             for s in range(SLABS):
                 bank = xt_psum.tile([P, CHUNK], F32, tag="xt", name="bank_a")
                 transpose_slab(nc, bank, x_chunks[c], s, ident)
-                if s < V_SLABS:
+                if s < 2:
                     for h in range(halves):
                         nc.vector.bn_stats(
                             out=bn_parts[:, s, c * halves + h, :],
                             in_=bank[:].bitcast(BF16)[:, h * BN_WIDTH : (h + 1) * BN_WIDTH],
                         )
                 else:
+                    u = s - 2
                     if c == 0:
-                        nc.scalar.mul(out=neg_x0[:], in_=bank[:].bitcast(BF16)[:, 0:2], mul=-1.0)
+                        nc.scalar.mul(
+                            out=neg_x0[:, 2 * u : 2 * u + 2],
+                            in_=bank[:].bitcast(BF16)[:, 0:2],
+                            mul=-1.0,
+                        )
                     for e in range(2):
-                        for func, parts in ((ACT.Identity, d_parts), (ACT.Square, dd_parts)):
-                            junk = junk_pool.tile([P, CHUNK], BF16, name="junk")
-                            nc.scalar.activation(
-                                out=junk[:],
-                                in_=half(bank, e),
-                                func=func,
-                                bias=neg_x0[:, e : e + 1],
-                                scale=1.0,
-                                accum_out=parts[:, e, c : c + 1],
-                            )
+                        junk = junk_pool.tile([P, CHUNK], BF16, name="junk")
+                        nc.scalar.activation(
+                            out=junk[:],
+                            in_=half(bank, e),
+                            func=ACT.Square,
+                            bias=neg_x0[:, 2 * u + e : 2 * u + e + 1],
+                            scale=1.0,
+                            accum_out=sq_parts[:, 2 * u + e, c : c + 1],
+                        )
+            for v in range(4):
+                first = CHANNELS // 2 + 256 * (v // 2) + v % 2
+                for j in range(ROW_TILES):
+                    nc.tensor.matmul(
+                        out=sum_parts[:, v, c : c + 1],
+                        lhsT=x_chunks[c][:, j, first : first + 255 : 2],
+                        rhs=ones[:],
+                        start=(j == 0),
+                        stop=(j == ROW_TILES - 1),
+                    )
 
         mean_var = keep.tile([P, PLANES, 2], F32, name="mean_var")
-        for s in range(V_SLABS):
+        for s in range(2):
             for e in range(2):
                 nc.vector.bn_aggr(
                     out=mean_var[:, 2 * s + e, :], in_=bn_parts[:, s, :, 3 * e : 3 * e + 3]
                 )
-        d_mean = keep.tile([P, 2], F32, name="d_mean")
-        dd_mean = keep.tile([P, 2], F32, name="dd_mean")
-        nc.vector.tensor_reduce(out=d_mean[:], in_=d_parts[:], axis=mybir.AxisListType.X, op=ALU.add)
-        nc.vector.tensor_reduce(out=dd_mean[:], in_=dd_parts[:], axis=mybir.AxisListType.X, op=ALU.add)
-        nc.vector.tensor_scalar_mul(out=d_mean[:], in0=d_mean[:], scalar1=1.0 / BATCH)
-        nc.vector.tensor_sub(out=mean_var[:, 2 * V_SLABS :, 0], in0=d_mean[:], in1=neg_x0[:])
-        nc.vector.tensor_mul(out=d_mean[:], in0=d_mean[:], in1=d_mean[:])
+        x_sum = keep.tile([P, 4], F32, name="x_sum")
+        sq_sum = keep.tile([P, 4], F32, name="sq_sum")
+        nc.vector.tensor_reduce(out=x_sum[:], in_=sum_parts[:], axis=mybir.AxisListType.X, op=ALU.add)
+        nc.vector.tensor_reduce(out=sq_sum[:], in_=sq_parts[:], axis=mybir.AxisListType.X, op=ALU.add)
+        nc.vector.tensor_scalar_mul(out=mean_var[:, 4:8, 0], in0=x_sum[:], scalar1=1.0 / BATCH)
+        off = keep.tile([P, 4], F32, name="off")
+        nc.vector.tensor_add(out=off[:], in0=mean_var[:, 4:8, 0], in1=neg_x0[:])
+        nc.vector.tensor_mul(out=off[:], in0=off[:], in1=off[:])
         nc.vector.scalar_tensor_tensor(
-            out=mean_var[:, 2 * V_SLABS :, 1],
-            in0=dd_mean[:],
+            out=mean_var[:, 4:8, 1],
+            in0=sq_sum[:],
             scalar=1.0 / BATCH,
-            in1=d_mean[:],
+            in1=off[:],
             op0=ALU.mult,
             op1=ALU.subtract,
         )
@@ -189,15 +206,25 @@ def tile_roibaseline_pa_t_kernel(tc, h_enc, enc_gamma, enc_beta, w1, b1, out):
                             bias=shift[:, 2 * s + e : 2 * s + e + 1],
                             scale=scale[:, 2 * s + e : 2 * s + e + 1],
                         )
+                pairs = c_pool.tile([P, 2, CHUNK, 2], BF16, name="pairs")
+                for u in range(2):
+                    y_by_row = y[:, 2 * u : 2 * u + 2, :].rearrange("p e b -> p b e")
+                    nc.vector.scalar_tensor_tensor(
+                        out=pairs[:, u, :, :],
+                        in0=y_by_row,
+                        scalar=SLOPE,
+                        in1=y_by_row,
+                        op0=ALU.mult,
+                        op1=ALU.max,
+                    )
                 grouped = c_pool.tile([P, CHUNK, 4], BF16, name="grouped", align_bytes=64)
-                y_by_row = y[:].rearrange("p t b -> p b t")
-                nc.vector.scalar_tensor_tensor(
-                    out=grouped[:],
-                    in0=y_by_row,
-                    scalar=SLOPE,
-                    in1=y_by_row,
-                    op0=ALU.mult,
-                    op1=ALU.max,
+                nc.vector.tensor_copy(
+                    out=grouped[:].rearrange("p b t -> p (b t)").bitcast(F32).rearrange(
+                        "p (b u) -> p b u", u=2
+                    ),
+                    in_=pairs[:].rearrange("p u b e -> p (u b e)").bitcast(F32).rearrange(
+                        "p (u b) -> p b u", u=2
+                    ),
                 )
                 nc.vector.quantize_mx(
                     out=codes[:, g, :].bitcast(FP8X4),

@@ -10,6 +10,7 @@ U8 = mybir.dt.uint8
 FP8X4 = mybir.dt.float8_e4m3fn_x4
 ALU = mybir.AluOpType
 ACT = mybir.ActivationFunctionType
+AXIS_X = mybir.AxisListType.X
 
 P = 128
 BATCH = 8192
@@ -24,10 +25,15 @@ CHUNKS = BATCH // CHUNK
 WORDS = CHANNELS // 2
 SLABS = WORDS // P
 PASSES = 2
-PLANES = 2 * SLABS
 BN_WIDTH = 512
+BN_CALLS = 2 * CHUNK // BN_WIDTH
+BN_SLOTS = CHUNKS * BN_CALLS
 
 FLOPS = 2 * BATCH * CHANNELS * FEATURES
+
+
+def scalar_takes(c, s):
+    return s == 3 or (s == 2 and c % 2 == 0)
 
 
 def transpose_slab(nc, bank, x_chunk, slab, ident):
@@ -60,25 +66,11 @@ def tile_roibaseline_pa_t_kernel(tc, h_enc, enc_gamma, enc_beta, w1, b1, out):
         make_identity(nc, ident[:])
         ones = keep.tile([P, 1], BF16, name="ones")
         nc.vector.memset(ones[:], 1.0)
-        warm = keep.tile([P, 1], F32, name="warm")
-        nc.vector.memset(warm[:], 1.0)
-        nc.scalar.activation(out=warm[:], in_=warm[:], func=ACT.Sqrt)
+        minus_half = keep.tile([P, 4], F32, name="minus_half")
+        nc.vector.memset(minus_half[:], -0.5)
 
         w_rows = keep.tile([P, CHANNELS], BF16, name="w_rows")
         nc.scalar.dma_start(out=w_rows[:], in_=w1)
-        gamma_bf = keep.tile([P, SLABS, 2], BF16, name="gamma_bf")
-        beta_bf = keep.tile([P, SLABS, 2], BF16, name="beta_bf")
-        nc.scalar.dma_start(
-            out=gamma_bf[:],
-            in_=enc_gamma.rearrange("r o -> (r o)").rearrange("(s p e) -> p s e", s=SLABS, p=P),
-        )
-        nc.scalar.dma_start(
-            out=beta_bf[:],
-            in_=enc_beta.rearrange("r o -> (r o)").rearrange("(s p e) -> p s e", s=SLABS, p=P),
-        )
-        bias_bf = keep.tile([P, FEATURES], BF16, name="bias_bf")
-        nc.scalar.dma_start(out=bias_bf[:], in_=b1.partition_broadcast(P))
-
         x_chunks = []
         for c in range(CHUNKS):
             x_chunk = keep.tile([P, ROW_TILES, CHANNELS], BF16, name="x%d" % c)
@@ -89,13 +81,18 @@ def tile_roibaseline_pa_t_kernel(tc, h_enc, enc_gamma, enc_beta, w1, b1, out):
                 ),
             )
             x_chunks.append(x_chunk)
-
-        gamma = keep.tile([P, PLANES], F32, name="gamma")
-        beta = keep.tile([P, PLANES], F32, name="beta")
-        bias = keep.tile([P, FEATURES], F32, name="bias")
-        nc.vector.tensor_copy(out=gamma[:], in_=gamma_bf[:].rearrange("p s e -> p (s e)"))
-        nc.vector.tensor_copy(out=beta[:], in_=beta_bf[:].rearrange("p s e -> p (s e)"))
-        nc.vector.tensor_copy(out=bias[:], in_=bias_bf[:])
+        gamma_bf = keep.tile([P, SLABS, 2], BF16, name="gamma_bf")
+        beta_bf = keep.tile([P, SLABS, 2], BF16, name="beta_bf")
+        bias_bf = keep.tile([P, FEATURES], BF16, name="bias_bf")
+        nc.sync.dma_start(
+            out=gamma_bf[:],
+            in_=enc_gamma.rearrange("r o -> (r o)").rearrange("(s p e) -> p s e", s=SLABS, p=P),
+        )
+        nc.sync.dma_start(
+            out=beta_bf[:],
+            in_=enc_beta.rearrange("r o -> (r o)").rearrange("(s p e) -> p s e", s=SLABS, p=P),
+        )
+        nc.sync.dma_start(out=bias_bf[:], in_=b1.partition_broadcast(P))
 
         w_bank = xt_psum.tile([P, SLABS * P], F32, tag="xt", name="w_bank")
         for s in range(SLABS):
@@ -113,81 +110,103 @@ def tile_roibaseline_pa_t_kernel(tc, h_enc, enc_gamma, enc_beta, w1, b1, out):
         w_scales = keep.tile([P, PASSES * FEATURES], U8, name="w_scales", align_bytes=64)
         nc.vector.quantize_mx(out=w_codes[:].bitcast(FP8X4), scales=w_scales[:], in_=w_grouped[:])
 
-        halves = CHUNK * 2 // BN_WIDTH
-        bn_parts = keep.tile([P, 2, CHUNKS * halves, 6], F32, name="bn_parts")
-        neg_x0 = keep.tile([P, 4], F32, name="neg_x0")
-        sq_parts = keep.tile([P, 4, CHUNKS], F32, name="sq_parts")
-        sum_parts = sum_psum.tile([P, 4, CHUNKS], F32, name="sum_parts")
+        bn_parts = keep.tile([P, SLABS, 1 + BN_SLOTS, 6], F32, name="bn_parts")
+        neg_x0 = keep.tile([P, 2, 2], F32, name="neg_x0")
+        sq_parts = keep.tile([P, 2, 2, CHUNKS], F32, name="sq_parts")
+        sum_parts = sum_psum.tile([P, 2, 2, CHUNKS], F32, name="sum_parts")
+        bn_used = [1, 1, 1, 1]
         for c in range(CHUNKS):
             for s in range(SLABS):
                 bank = xt_psum.tile([P, CHUNK], F32, tag="xt", name="bank_a")
                 transpose_slab(nc, bank, x_chunks[c], s, ident)
-                if s < 2:
-                    for h in range(halves):
+                if not scalar_takes(c, s):
+                    for h in range(BN_CALLS):
                         nc.vector.bn_stats(
-                            out=bn_parts[:, s, c * halves + h, :],
+                            out=bn_parts[:, s, bn_used[s], :],
                             in_=bank[:].bitcast(BF16)[:, h * BN_WIDTH : (h + 1) * BN_WIDTH],
                         )
-                else:
-                    u = s - 2
-                    if c == 0:
-                        nc.scalar.mul(
-                            out=neg_x0[:, 2 * u : 2 * u + 2],
-                            in_=bank[:].bitcast(BF16)[:, 0:2],
-                            mul=-1.0,
-                        )
-                    for e in range(2):
-                        junk = junk_pool.tile([P, CHUNK], BF16, name="junk")
-                        nc.scalar.activation(
-                            out=junk[:],
-                            in_=half(bank, e),
-                            func=ACT.Square,
-                            bias=neg_x0[:, 2 * u + e : 2 * u + e + 1],
-                            scale=1.0,
-                            accum_out=sq_parts[:, 2 * u + e, c : c + 1],
-                        )
-            for v in range(4):
-                first = CHANNELS // 2 + 256 * (v // 2) + v % 2
-                for j in range(ROW_TILES):
-                    nc.tensor.matmul(
-                        out=sum_parts[:, v, c : c + 1],
-                        lhsT=x_chunks[c][:, j, first : first + 255 : 2],
-                        rhs=ones[:],
-                        start=(j == 0),
-                        stop=(j == ROW_TILES - 1),
+                        bn_used[s] += 1
+                    continue
+                u = s - 2
+                if c == 0:
+                    nc.scalar.mul(
+                        out=neg_x0[:, u, :], in_=bank[:].bitcast(BF16)[:, 0:2], mul=-1.0
                     )
+                for e in range(2):
+                    junk = junk_pool.tile([P, CHUNK], BF16, name="junk")
+                    nc.scalar.activation(
+                        out=junk[:],
+                        in_=half(bank, e),
+                        func=ACT.Square,
+                        bias=neg_x0[:, u, e : e + 1],
+                        scale=1.0,
+                        accum_out=sq_parts[:, u, e, c : c + 1],
+                    )
+                    first = 256 * s + e
+                    for j in range(ROW_TILES):
+                        nc.tensor.matmul(
+                            out=sum_parts[:, u, e, c : c + 1],
+                            lhsT=x_chunks[c][:, j, first : first + 255 : 2],
+                            rhs=ones[:],
+                            start=(j == 0),
+                            stop=(j == ROW_TILES - 1),
+                        )
 
-        mean_var = keep.tile([P, PLANES, 2], F32, name="mean_var")
-        for s in range(2):
-            for e in range(2):
+        gamma = keep.tile([P, SLABS * 2], F32, name="gamma")
+        beta = keep.tile([P, SLABS * 2], F32, name="beta")
+        bias = keep.tile([P, FEATURES], F32, name="bias")
+        nc.vector.tensor_copy(out=gamma[:], in_=gamma_bf[:].rearrange("p s e -> p (s e)"))
+        nc.vector.tensor_copy(out=beta[:], in_=beta_bf[:].rearrange("p s e -> p (s e)"))
+        nc.vector.tensor_copy(out=bias[:], in_=bias_bf[:])
+
+        def scale_and_shift(g):
+            mean_var = keep.tile([P, 4, 2], F32, name="mean_var%d" % g)
+            for t in range(4):
+                s = 2 * g + t // 2
+                e = t % 2
+                first_slot = 0 if s >= 2 else 1
                 nc.vector.bn_aggr(
-                    out=mean_var[:, 2 * s + e, :], in_=bn_parts[:, s, :, 3 * e : 3 * e + 3]
+                    out=mean_var[:, t, :],
+                    in_=bn_parts[:, s, first_slot : bn_used[s], 3 * e : 3 * e + 3],
                 )
-        x_sum = keep.tile([P, 4], F32, name="x_sum")
-        sq_sum = keep.tile([P, 4], F32, name="sq_sum")
-        nc.vector.tensor_reduce(out=x_sum[:], in_=sum_parts[:], axis=mybir.AxisListType.X, op=ALU.add)
-        nc.vector.tensor_reduce(out=sq_sum[:], in_=sq_parts[:], axis=mybir.AxisListType.X, op=ALU.add)
-        nc.vector.tensor_scalar_mul(out=mean_var[:, 4:8, 0], in0=x_sum[:], scalar1=1.0 / BATCH)
-        off = keep.tile([P, 4], F32, name="off")
-        nc.vector.tensor_add(out=off[:], in0=mean_var[:, 4:8, 0], in1=neg_x0[:])
-        nc.vector.tensor_mul(out=off[:], in0=off[:], in1=off[:])
-        nc.vector.scalar_tensor_tensor(
-            out=mean_var[:, 4:8, 1],
-            in0=sq_sum[:],
-            scalar=1.0 / BATCH,
-            in1=off[:],
-            op0=ALU.mult,
-            op1=ALU.subtract,
-        )
-        std = keep.tile([P, PLANES], F32, name="std")
-        nc.vector.tensor_scalar_add(out=std[:], in0=mean_var[:, :, 1], scalar1=EPS)
-        nc.scalar.activation(out=std[:], in_=std[:], func=ACT.Sqrt)
-        scale = keep.tile([P, PLANES], F32, name="scale")
-        shift = keep.tile([P, PLANES], F32, name="shift")
-        nc.vector.reciprocal(out=scale[:], in_=std[:])
-        nc.vector.tensor_mul(out=scale[:], in0=scale[:], in1=gamma[:])
-        nc.vector.tensor_mul(out=shift[:], in0=mean_var[:, :, 0], in1=scale[:])
-        nc.vector.tensor_sub(out=shift[:], in0=beta[:], in1=shift[:])
+            scale = keep.tile([P, 4], F32, name="scale%d" % g)
+            shift = keep.tile([P, 4], F32, name="shift%d" % g)
+            nc.vector.tensor_scalar_add(out=scale[:], in0=mean_var[:, :, 1], scalar1=EPS)
+            nc.gpsimd.tensor_tensor(out=scale[:], in0=scale[:], in1=minus_half[:], op=ALU.pow)
+            nc.vector.tensor_mul(out=scale[:], in0=scale[:], in1=gamma[:, 4 * g : 4 * g + 4])
+            nc.vector.tensor_mul(out=shift[:], in0=mean_var[:, :, 0], in1=scale[:])
+            nc.vector.tensor_sub(out=shift[:], in0=beta[:, 4 * g : 4 * g + 4], in1=shift[:])
+            return scale, shift
+
+        affine = [scale_and_shift(0)]
+
+        x_sum = keep.tile([P, 2, 2], F32, name="x_sum")
+        sq_sum = keep.tile([P, 2, 2], F32, name="sq_sum")
+        off = keep.tile([P, 2, 2], F32, name="off")
+        for u in range(2):
+            step = 2 - u
+            rows = float(BATCH // step)
+            share = bn_parts[:, 2 + u, 0, :].rearrange("p (e k) -> p e k", k=3)
+            nc.vector.memset(share[:, :, 0], rows)
+            nc.vector.tensor_reduce(
+                out=x_sum[:, u, :], in_=sum_parts[:, u, :, 0:CHUNKS:step], axis=AXIS_X, op=ALU.add
+            )
+            nc.vector.tensor_reduce(
+                out=sq_sum[:, u, :], in_=sq_parts[:, u, :, 0:CHUNKS:step], axis=AXIS_X, op=ALU.add
+            )
+            nc.vector.tensor_scalar_mul(out=share[:, :, 1], in0=x_sum[:, u, :], scalar1=1.0 / rows)
+            nc.vector.tensor_add(out=off[:, u, :], in0=share[:, :, 1], in1=neg_x0[:, u, :])
+            nc.vector.tensor_mul(out=off[:, u, :], in0=off[:, u, :], in1=off[:, u, :])
+            nc.vector.scalar_tensor_tensor(
+                out=share[:, :, 2],
+                in0=off[:, u, :],
+                scalar=-rows,
+                in1=sq_sum[:, u, :],
+                op0=ALU.mult,
+                op1=ALU.add,
+            )
+
+        affine.append(scale_and_shift(1))
 
         for c in range(CHUNKS):
             codes = q_pool.tile([P, PASSES, CHUNK], U32, name="codes", align_bytes=64)
@@ -195,16 +214,16 @@ def tile_roibaseline_pa_t_kernel(tc, h_enc, enc_gamma, enc_beta, w1, b1, out):
             for g in range(PASSES):
                 y = y_pool.tile([P, 4, CHUNK], F32, name="y")
                 for u in range(2):
-                    s = 2 * g + u
                     bank = xt_psum.tile([P, CHUNK], F32, tag="xt", name="bank_b")
-                    transpose_slab(nc, bank, x_chunks[c], s, ident)
+                    transpose_slab(nc, bank, x_chunks[c], 2 * g + u, ident)
                     for e in range(2):
+                        t = 2 * u + e
                         nc.scalar.activation(
-                            out=y[:, 2 * u + e, :],
+                            out=y[:, t, :],
                             in_=half(bank, e),
                             func=ACT.Identity,
-                            bias=shift[:, 2 * s + e : 2 * s + e + 1],
-                            scale=scale[:, 2 * s + e : 2 * s + e + 1],
+                            bias=affine[g][1][:, t : t + 1],
+                            scale=affine[g][0][:, t : t + 1],
                         )
                 pairs = c_pool.tile([P, 2, CHUNK, 2], BF16, name="pairs")
                 for u in range(2):

@@ -58,8 +58,9 @@ def tile_roibaseline_pa_t_kernel(tc, h_enc, enc_gamma, enc_beta, w1, b1, out):
         c_pool = ctx.enter_context(tc.tile_pool(name="c", bufs=3))
         q_pool = ctx.enter_context(tc.tile_pool(name="q", bufs=3))
         o_pool = ctx.enter_context(tc.tile_pool(name="o", bufs=3))
-        xt_psum = ctx.enter_context(tc.psum_pool(name="xt", bufs=5))
+        xt_psum = ctx.enter_context(tc.psum_pool(name="xt", bufs=4))
         acc_psum = ctx.enter_context(tc.psum_pool(name="acc", bufs=2))
+        back_psum = ctx.enter_context(tc.psum_pool(name="back", bufs=1))
         sum_psum = ctx.enter_context(tc.psum_pool(name="sum", bufs=1))
 
         ident = keep.tile([P, P], F32, name="ident")
@@ -83,7 +84,7 @@ def tile_roibaseline_pa_t_kernel(tc, h_enc, enc_gamma, enc_beta, w1, b1, out):
             x_chunks.append(x_chunk)
         gamma_bf = keep.tile([P, SLABS, 2], BF16, name="gamma_bf")
         beta_bf = keep.tile([P, SLABS, 2], BF16, name="beta_bf")
-        bias_bf = keep.tile([P, FEATURES], BF16, name="bias_bf")
+        bias_bf = keep.tile([P, 1], BF16, name="bias_bf")
         nc.sync.dma_start(
             out=gamma_bf[:],
             in_=enc_gamma.rearrange("r o -> (r o)").rearrange("(s p e) -> p s e", s=SLABS, p=P),
@@ -92,7 +93,7 @@ def tile_roibaseline_pa_t_kernel(tc, h_enc, enc_gamma, enc_beta, w1, b1, out):
             out=beta_bf[:],
             in_=enc_beta.rearrange("r o -> (r o)").rearrange("(s p e) -> p s e", s=SLABS, p=P),
         )
-        nc.sync.dma_start(out=bias_bf[:], in_=b1.partition_broadcast(P))
+        nc.sync.dma_start(out=bias_bf[:], in_=b1.rearrange("(f o) -> f o", o=1))
 
         w_bank = xt_psum.tile([P, SLABS * P], F32, tag="xt", name="w_bank")
         for s in range(SLABS):
@@ -154,7 +155,7 @@ def tile_roibaseline_pa_t_kernel(tc, h_enc, enc_gamma, enc_beta, w1, b1, out):
 
         gamma = keep.tile([P, SLABS * 2], F32, name="gamma")
         beta = keep.tile([P, SLABS * 2], F32, name="beta")
-        bias = keep.tile([P, FEATURES], F32, name="bias")
+        bias = keep.tile([P, 1], F32, name="bias")
         nc.vector.tensor_copy(out=gamma[:], in_=gamma_bf[:].rearrange("p s e -> p (s e)"))
         nc.vector.tensor_copy(out=beta[:], in_=beta_bf[:].rearrange("p s e -> p (s e)"))
         nc.vector.tensor_copy(out=bias[:], in_=bias_bf[:])
@@ -250,26 +251,29 @@ def tile_roibaseline_pa_t_kernel(tc, h_enc, enc_gamma, enc_beta, w1, b1, out):
                     scales=scales[:, g, :],
                     in_=grouped[:].rearrange("p b t -> p (b t)"),
                 )
-            acc = acc_psum.tile([P, ROW_TILES, FEATURES], F32, name="acc")
-            for j in range(ROW_TILES):
-                rows = slice(j * P, (j + 1) * P)
-                for g in range(PASSES):
-                    cols = slice(g * FEATURES, (g + 1) * FEATURES)
-                    nc.tensor.matmul_mx(
-                        out=acc[:, j, :],
-                        lhsT=codes[:, g, rows].bitcast(FP8X4),
-                        lhsT_scale=scales[:, g, rows],
-                        rhs=w_codes[:, cols].bitcast(FP8X4),
-                        rhs_scale=w_scales[:, cols],
-                        start=(g == 0),
-                        stop=(g == PASSES - 1),
-                    )
-            result = o_pool.tile([P, ROW_TILES, FEATURES], F32, name="result")
-            nc.vector.tensor_add(
-                out=result[:],
-                in0=acc[:],
-                in1=bias[:].unsqueeze(1).to_broadcast([P, ROW_TILES, FEATURES]),
+            acc = acc_psum.tile([P, CHUNK], F32, name="acc")
+            for g in range(PASSES):
+                cols = slice(g * FEATURES, (g + 1) * FEATURES)
+                nc.tensor.matmul_mx(
+                    out=acc[:],
+                    lhsT=w_codes[:, cols].bitcast(FP8X4),
+                    lhsT_scale=w_scales[:, cols],
+                    rhs=codes[:, g, :].bitcast(FP8X4),
+                    rhs_scale=scales[:, g, :],
+                    start=(g == 0),
+                    stop=(g == PASSES - 1),
+                )
+            by_feature = o_pool.tile([P, CHUNK], F32, name="by_feature")
+            nc.scalar.activation(
+                out=by_feature[:], in_=acc[:], func=ACT.Identity, bias=bias[:], scale=1.0
             )
+            back = back_psum.tile([P, ROW_TILES, FEATURES], F32, name="back")
+            for j in range(ROW_TILES):
+                nc.tensor.transpose(
+                    out=back[:, j, :], in_=by_feature[:, j * P : (j + 1) * P], identity=ident[:]
+                )
+            result = o_pool.tile([P, ROW_TILES, FEATURES], F32, name="result")
+            nc.scalar.copy(out=result[:], in_=back[:])
             nc.sync.dma_start(
                 out=out[c * CHUNK : (c + 1) * CHUNK, :].rearrange("(p j) f -> p j f", j=ROW_TILES),
                 in_=result[:],

from contextlib import ExitStack

import concourse.mybir as mybir
from concourse.masks import make_identity

F32 = mybir.dt.float32
BF16 = mybir.dt.bfloat16
U32 = mybir.dt.uint32
U8 = mybir.dt.uint8
FP8X4 = mybir.dt.float8_e4m3fn_x4
ALU = mybir.AluOpType
ACT = mybir.ActivationFunctionType
AXIS_X = mybir.AxisListType.X

P = 128
BATCH = 8192
CHANNELS = 1024
FEATURES = 128
EPS = 1e-5
SLOPE = 0.3

ROW_TILES = 4
CHUNK = P * ROW_TILES
CHUNKS = BATCH // CHUNK
WORDS = CHANNELS // 2
SLABS = WORDS // P
PASSES = 2
BN_WIDTH = 512
BN_CALLS = 2 * CHUNK // BN_WIDTH
BN_SLOTS = CHUNKS * BN_CALLS

FLOPS = 2 * BATCH * CHANNELS * FEATURES


def scalar_takes(c, s):
    return s == 3 or (s == 2 and c % 2 == 0)


def transpose_slab(nc, bank, x_chunk, slab, ident):
    for j in range(ROW_TILES):
        nc.tensor.transpose(
            out=bank[:, j * P : (j + 1) * P],
            in_=x_chunk[:, j, :].bitcast(F32)[:, slab * P : (slab + 1) * P],
            identity=ident[:],
        )


def half(bank, e):
    return bank[:].bitcast(BF16).rearrange("p (b e) -> p b e", e=2)[:, :, e]


def tile_roibaseline_pa_t_kernel(tc, h_enc, enc_gamma, enc_beta, w1, b1, out):
    nc = tc.nc
    with ExitStack() as ctx:
        keep = ctx.enter_context(tc.tile_pool(name="keep", bufs=1))
        junk_pool = ctx.enter_context(tc.tile_pool(name="junk", bufs=4))
        y_pool = ctx.enter_context(tc.tile_pool(name="y", bufs=3))
        c_pool = ctx.enter_context(tc.tile_pool(name="c", bufs=3))
        q_pool = ctx.enter_context(tc.tile_pool(name="q", bufs=3))
        o_pool = ctx.enter_context(tc.tile_pool(name="o", bufs=3))
        xt_psum = ctx.enter_context(tc.psum_pool(name="xt", bufs=4))
        acc_psum = ctx.enter_context(tc.psum_pool(name="acc", bufs=2))
        back_psum = ctx.enter_context(tc.psum_pool(name="back", bufs=1))
        sum_psum = ctx.enter_context(tc.psum_pool(name="sum", bufs=1))

        ident = keep.tile([P, P], F32, name="ident")
        make_identity(nc, ident[:])
        ones = keep.tile([P, 1], BF16, name="ones")
        nc.vector.memset(ones[:], 1.0)
        minus_half = keep.tile([P, 4], F32, name="minus_half")
        nc.vector.memset(minus_half[:], -0.5)

        w_rows = keep.tile([P, CHANNELS], BF16, name="w_rows")
        nc.scalar.dma_start(out=w_rows[:], in_=w1)
        x_chunks = []
        for c in range(CHUNKS):
            x_chunk = keep.tile([P, ROW_TILES, CHANNELS], BF16, name="x%d" % c)
            nc.sync.dma_start(
                out=x_chunk[:],
                in_=h_enc[c * CHUNK : (c + 1) * CHUNK].rearrange(
                    "(p j) r o -> p j (r o)", j=ROW_TILES
                ),
            )
            x_chunks.append(x_chunk)
        gamma_bf = keep.tile([P, SLABS, 2], BF16, name="gamma_bf")
        beta_bf = keep.tile([P, SLABS, 2], BF16, name="beta_bf")
        bias_bf = keep.tile([P, 1], BF16, name="bias_bf")
        nc.sync.dma_start(
            out=gamma_bf[:],
            in_=enc_gamma.rearrange("r o -> (r o)").rearrange("(s p e) -> p s e", s=SLABS, p=P),
        )
        nc.sync.dma_start(
            out=beta_bf[:],
            in_=enc_beta.rearrange("r o -> (r o)").rearrange("(s p e) -> p s e", s=SLABS, p=P),
        )
        nc.sync.dma_start(out=bias_bf[:], in_=b1.rearrange("(f o) -> f o", o=1))

        w_bank = xt_psum.tile([P, SLABS * P], F32, tag="xt", name="w_bank")
        for s in range(SLABS):
            nc.tensor.transpose(
                out=w_bank[:, s * P : (s + 1) * P],
                in_=w_rows[:].bitcast(F32)[:, s * P : (s + 1) * P],
                identity=ident[:],
            )
        w_grouped = keep.tile([P, PASSES * FEATURES * 4], BF16, name="w_grouped", align_bytes=64)
        nc.vector.tensor_copy(
            out=w_grouped[:].bitcast(F32).rearrange("p (g f u) -> p g f u", g=PASSES, u=2),
            in_=w_bank[:].rearrange("p (g u f) -> p g f u", g=PASSES, u=2),
        )
        w_codes = keep.tile([P, PASSES * FEATURES], U32, name="w_codes", align_bytes=64)
        w_scales = keep.tile([P, PASSES * FEATURES], U8, name="w_scales", align_bytes=64)
        nc.vector.quantize_mx(out=w_codes[:].bitcast(FP8X4), scales=w_scales[:], in_=w_grouped[:])

        bn_parts = keep.tile([P, SLABS, 1 + BN_SLOTS, 6], F32, name="bn_parts")
        neg_x0 = keep.tile([P, 2, 2], F32, name="neg_x0")
        sq_parts = keep.tile([P, 2, 2, CHUNKS], F32, name="sq_parts")
        sum_parts = sum_psum.tile([P, 2, 2, CHUNKS], F32, name="sum_parts")
        bn_used = [1, 1, 1, 1]
        for c in range(CHUNKS):
            for s in range(SLABS):
                bank = xt_psum.tile([P, CHUNK], F32, tag="xt", name="bank_a")
                transpose_slab(nc, bank, x_chunks[c], s, ident)
                if not scalar_takes(c, s):
                    for h in range(BN_CALLS):
                        nc.vector.bn_stats(
                            out=bn_parts[:, s, bn_used[s], :],
                            in_=bank[:].bitcast(BF16)[:, h * BN_WIDTH : (h + 1) * BN_WIDTH],
                        )
                        bn_used[s] += 1
                    continue
                u = s - 2
                if c == 0:
                    nc.scalar.mul(
                        out=neg_x0[:, u, :], in_=bank[:].bitcast(BF16)[:, 0:2], mul=-1.0
                    )
                for e in range(2):
                    junk = junk_pool.tile([P, CHUNK], BF16, name="junk")
                    nc.scalar.activation(
                        out=junk[:],
                        in_=half(bank, e),
                        func=ACT.Square,
                        bias=neg_x0[:, u, e : e + 1],
                        scale=1.0,
                        accum_out=sq_parts[:, u, e, c : c + 1],
                    )
                    first = 256 * s + e
                    for j in range(ROW_TILES):
                        nc.tensor.matmul(
                            out=sum_parts[:, u, e, c : c + 1],
                            lhsT=x_chunks[c][:, j, first : first + 255 : 2],
                            rhs=ones[:],
                            start=(j == 0),
                            stop=(j == ROW_TILES - 1),
                        )

        gamma = keep.tile([P, SLABS * 2], F32, name="gamma")
        beta = keep.tile([P, SLABS * 2], F32, name="beta")
        bias = keep.tile([P, 1], F32, name="bias")
        nc.vector.tensor_copy(out=gamma[:], in_=gamma_bf[:].rearrange("p s e -> p (s e)"))
        nc.vector.tensor_copy(out=beta[:], in_=beta_bf[:].rearrange("p s e -> p (s e)"))
        nc.vector.tensor_copy(out=bias[:], in_=bias_bf[:])

        def scale_and_shift(g):
            mean_var = keep.tile([P, 4, 2], F32, name="mean_var%d" % g)
            for t in range(4):
                s = 2 * g + t // 2
                e = t % 2
                first_slot = 0 if s >= 2 else 1
                nc.vector.bn_aggr(
                    out=mean_var[:, t, :],
                    in_=bn_parts[:, s, first_slot : bn_used[s], 3 * e : 3 * e + 3],
                )
            scale = keep.tile([P, 4], F32, name="scale%d" % g)
            shift = keep.tile([P, 4], F32, name="shift%d" % g)
            nc.vector.tensor_scalar_add(out=scale[:], in0=mean_var[:, :, 1], scalar1=EPS)
            nc.gpsimd.tensor_tensor(out=scale[:], in0=scale[:], in1=minus_half[:], op=ALU.pow)
            nc.vector.tensor_mul(out=scale[:], in0=scale[:], in1=gamma[:, 4 * g : 4 * g + 4])
            nc.vector.tensor_mul(out=shift[:], in0=mean_var[:, :, 0], in1=scale[:])
            nc.vector.tensor_sub(out=shift[:], in0=beta[:, 4 * g : 4 * g + 4], in1=shift[:])
            return scale, shift

        affine = [scale_and_shift(0)]

        x_sum = keep.tile([P, 2, 2], F32, name="x_sum")
        sq_sum = keep.tile([P, 2, 2], F32, name="sq_sum")
        off = keep.tile([P, 2, 2], F32, name="off")
        for u in range(2):
            step = 2 - u
            rows = float(BATCH // step)
            share = bn_parts[:, 2 + u, 0, :].rearrange("p (e k) -> p e k", k=3)
            nc.vector.memset(share[:, :, 0], rows)
            nc.vector.tensor_reduce(
                out=x_sum[:, u, :], in_=sum_parts[:, u, :, 0:CHUNKS:step], axis=AXIS_X, op=ALU.add
            )
            nc.vector.tensor_reduce(
                out=sq_sum[:, u, :], in_=sq_parts[:, u, :, 0:CHUNKS:step], axis=AXIS_X, op=ALU.add
            )
            nc.vector.tensor_scalar_mul(out=share[:, :, 1], in0=x_sum[:, u, :], scalar1=1.0 / rows)
            nc.vector.tensor_add(out=off[:, u, :], in0=share[:, :, 1], in1=neg_x0[:, u, :])
            nc.vector.tensor_mul(out=off[:, u, :], in0=off[:, u, :], in1=off[:, u, :])
            nc.vector.scalar_tensor_tensor(
                out=share[:, :, 2],
                in0=off[:, u, :],
                scalar=-rows,
                in1=sq_sum[:, u, :],
                op0=ALU.mult,
                op1=ALU.add,
            )

        affine.append(scale_and_shift(1))

        for c in range(CHUNKS):
            codes = q_pool.tile([P, PASSES, CHUNK], U32, name="codes", align_bytes=64)
            scales = q_pool.tile([P, PASSES, CHUNK], U8, name="scales", align_bytes=64)
            for g in range(PASSES):
                y = y_pool.tile([P, 4, CHUNK], F32, name="y")
                for u in range(2):
                    bank = xt_psum.tile([P, CHUNK], F32, tag="xt", name="bank_b")
                    transpose_slab(nc, bank, x_chunks[c], 2 * g + u, ident)
                    for e in range(2):
                        t = 2 * u + e
                        nc.scalar.activation(
                            out=y[:, t, :],
                            in_=half(bank, e),
                            func=ACT.Identity,
                            bias=affine[g][1][:, t : t + 1],
                            scale=affine[g][0][:, t : t + 1],
                        )
                pairs = c_pool.tile([P, 2, CHUNK, 2], BF16, name="pairs")
                for u in range(2):
                    y_by_row = y[:, 2 * u : 2 * u + 2, :].rearrange("p e b -> p b e")
                    nc.vector.scalar_tensor_tensor(
                        out=pairs[:, u, :, :],
                        in0=y_by_row,
                        scalar=SLOPE,
                        in1=y_by_row,
                        op0=ALU.mult,
                        op1=ALU.max,
                    )
                grouped = c_pool.tile([P, CHUNK, 4], BF16, name="grouped", align_bytes=64)
                nc.vector.tensor_copy(
                    out=grouped[:].rearrange("p b t -> p (b t)").bitcast(F32).rearrange(
                        "p (b u) -> p b u", u=2
                    ),
                    in_=pairs[:].rearrange("p u b e -> p (u b e)").bitcast(F32).rearrange(
                        "p (u b) -> p b u", u=2
                    ),
                )
                nc.vector.quantize_mx(
                    out=codes[:, g, :].bitcast(FP8X4),
                    scales=scales[:, g, :],
                    in_=grouped[:].rearrange("p b t -> p (b t)"),
                )
            acc = acc_psum.tile([P, CHUNK], F32, name="acc")
            for g in range(PASSES):
                cols = slice(g * FEATURES, (g + 1) * FEATURES)
                nc.tensor.matmul_mx(
                    out=acc[:],
                    lhsT=w_codes[:, cols].bitcast(FP8X4),
                    lhsT_scale=w_scales[:, cols],
                    rhs=codes[:, g, :].bitcast(FP8X4),
                    rhs_scale=scales[:, g, :],
                    start=(g == 0),
                    stop=(g == PASSES - 1),
                )
            by_feature = o_pool.tile([P, CHUNK], F32, name="by_feature")
            nc.scalar.activation(
                out=by_feature[:], in_=acc[:], func=ACT.Identity, bias=bias[:], scale=1.0
            )
            back = back_psum.tile([P, ROW_TILES, FEATURES], F32, name="back")
            for j in range(ROW_TILES):
                nc.tensor.transpose(
                    out=back[:, j, :], in_=by_feature[:, j * P : (j + 1) * P], identity=ident[:]
                )
            result = o_pool.tile([P, ROW_TILES, FEATURES], F32, name="result")
            nc.scalar.copy(out=result[:], in_=back[:])
            nc.sync.dma_start(
                out=out[c * CHUNK : (c + 1) * CHUNK, :].rearrange("(p j) f -> p j f", j=ROW_TILES),
                in_=result[:],
            )
